import numpy as np
import ml_dtypes


def mxq(x, axis, fmt="e4m3"):
    dtype, down = {"e4m3": (ml_dtypes.float8_e4m3fn, 7), "e5m2": (ml_dtypes.float8_e5m2, 14)}[fmt]
    v = np.moveaxis(np.asarray(x, np.float32).astype(ml_dtypes.bfloat16).astype(np.float64), axis, -1)
    blocks = v.reshape(v.shape[:-1] + (-1, 32))
    amax = np.abs(blocks).max(-1, keepdims=True)
    byte = np.maximum(np.where(amax > 0, np.frexp(amax)[1] - 1 + 127, 0) - down, 1)
    scale = np.exp2(byte - 127.0)
    codes = (blocks / scale).astype(np.float32).astype(dtype).astype(np.float64)
    return np.moveaxis((codes * scale).reshape(v.shape), -1, axis)


WIDE = False


def mx_kscale(k):
    if not WIDE:
        return np.ones(k)
    levels = np.array([10, -10, 5, -5, 0])
    if k % 512:
        return np.exp2(np.random.permutation(np.resize(levels, k // 32))).repeat(32)
    a = np.empty((k // 512, 16))
    for p in range(k // 512):
        a[p, :8] = np.random.permutation(np.resize(levels, 8))
        for g in range(8):
            far = levels[np.abs(levels - a[p, g]) >= 10]
            a[p, g + 8] = far[np.random.randint(len(far))]
    return np.exp2(a.ravel()).repeat(32)


BF16 = ml_dtypes.bfloat16


def bf(x):
    return np.asarray(x, np.float32).astype(BF16)


def f64(x):
    return np.asarray(x).astype(np.float64)


B, C, T, V, S = 4, 64, 16, 256, 4
O = C
K = S * V
EPS = 1e-5
ZS = 0.35


def setup_inputs():
    s = mx_kscale(K).reshape(S, V)
    z = (np.random.standard_normal((S, B, O, T, V)) + np.random.standard_normal(O)[None, None, :, None, None] / np.sqrt(K)) * ZS
    return {"z": bf(z * s[:, None, None, None, :]),
            "A": bf(np.random.uniform(size=(S, V, V)) / s[:, :, None]),
            "x": bf(np.random.standard_normal((B, C, T, V))),
            "gamma": bf(1.0 + 0.1 * np.random.standard_normal(O)),
            "beta": bf(0.1 * np.random.standard_normal(O))}


def reference(z, A, x, gamma, beta):
    x = f64(x)
    zk = np.moveaxis(f64(z), 0, 3).reshape(B, O, T, K)
    ak = f64(A).reshape(K, V)
    y = mxq(zk, 3, "e4m3") @ mxq(ak, 0, "e4m3")
    mean = y.mean(axis=(0, 2, 3), keepdims=True)
    var = y.var(axis=(0, 2, 3), keepdims=True)
    y_hat = (y - mean) / np.sqrt(var + EPS)
    y_bn = y_hat * f64(gamma)[None, :, None, None] + f64(beta)[None, :, None, None]
    return np.maximum(y_bn + x, 0.0)

@@ -1,0 +1,237 @@
+from contextlib import ExitStack
+
+import concourse.mybir as mybir
+from concourse.masks import make_identity
+
+FP8X4 = mybir.dt.float8_e4m3fn_x4
+BF16 = mybir.dt.bfloat16
+F32 = mybir.dt.float32
+U32 = mybir.dt.uint32
+U8 = mybir.dt.uint8
+ALU = mybir.AluOpType
+ACT = mybir.ActivationFunctionType
+
+S, B, O, T, V = 4, 4, 64, 16, 256
+P = 128
+EPS = 1e-5
+FLOPS = 2 * B * O * T * S * V * V
+
+TILES = B * O * T // P
+PAIRS = TILES // 2
+GROUP = 4
+T_BANKS = GROUP
+Y_BANKS = 7 - GROUP
+MISC_BANK = 7
+PIN = True
+
+
+def tile_dggcn_sparse_assemble_pa_kernel(tc, z, A, x, gamma, beta, out):
+    nc = tc.nc
+    with ExitStack() as ctx:
+        if PIN:
+            ctx.enter_context(tc.manual_schedule())
+        const = ctx.enter_context(tc.tile_pool(name="const", bufs=1))
+        keep = ctx.enter_context(tc.tile_pool(name="keep", bufs=1))
+        gpool = ctx.enter_context(tc.tile_pool(name="gpool", bufs=8))
+        rpool = ctx.enter_context(tc.tile_pool(name="rpool", bufs=4))
+        psum = ctx.enter_context(tc.psum_pool(name="psum", bufs=1))
+
+        zv = z.rearrange("s b o (th tl) v -> b s (o th) tl v", th=2)
+        xv = x.rearrange("b c (th tl) v -> b (c th) (tl v)", th=2)
+        ov = out.rearrange("b c (th tl) v -> b (c th) (tl v)", th=2)
+        av = A.rearrange("s v w -> (s v) w").rearrange("(g q t) w -> q g (t w)", q=P, t=4)
+
+        gb_rows = const.tile([P, 2 * O], BF16, name="gb_rows")
+        nc.vector.memset(gb_rows[:], 0.0)
+        nc.scalar.dma_start(out=gb_rows[0:1, 0:O], in_=gamma.rearrange("(u o) -> u o", u=1))
+        nc.scalar.dma_start(out=gb_rows[1:2, O:2 * O], in_=beta.rearrange("(u o) -> u o", u=1))
+
+        chunks = [2, 2] + [4] * (TILES // 4 - 1)
+        z_raw = [keep.tile([P, n, S, V], BF16, name="z_raw%d" % c) for c, n in enumerate(chunks)]
+        where = [(c, k) for c, n in enumerate(chunks) for k in range(n)]
+        a_raw = const.tile([P, 2 * S, V], BF16, name="a_raw")
+        x_sb = [keep.tile([P, 8 * V], BF16, name="x_sb%d" % b) for b in range(B)]
+
+        def load_z(c):
+            t0 = sum(chunks[:c])
+            tl = t0 % 8
+            for s in range(S):
+                nc.sync.dma_start(out=z_raw[c][:, :, s, :], in_=zv[t0 // 8, s, :, tl:tl + chunks[c], :])
+
+        load_z(0)
+        nc.sync.dma_start(out=a_raw[:].rearrange("q (g t) w -> q g (t w)", t=4), in_=av)
+        for c in range(1, len(chunks)):
+            load_z(c)
+        for b in (3, 0, 1, 2):
+            nc.sync.dma_start(out=x_sb[b][:], in_=xv[b])
+
+        ident = const.tile([P, P], F32, name="ident")
+        make_identity(nc, ident[:])
+        one = const.tile([P, 1], F32, name="one")
+        nc.vector.memset(one[:], 1.0)
+        warm = const.tile([P, 1], F32, name="warm")
+        nc.scalar.activation(out=warm[:], in_=one[:], func=ACT.Sqrt)
+        eps_t = const.tile([P, 1], F32, name="eps_t")
+        nc.vector.memset(eps_t[:], EPS)
+        idv = ident[:].rearrange("p (o r) -> p o r", r=2)
+        half = const.tile([P, O], F32, name="half")
+        nc.vector.tensor_tensor(out=half[:], in0=idv[:, :, 0], in1=idv[:, :, 1], op=ALU.add)
+        pair_avg = const.tile([P, O, 2], F32, name="pair_avg")
+        nc.vector.tensor_scalar(out=pair_avg[:], in0=half[:].unsqueeze(2).to_broadcast([P, O, 2]),
+                                scalar1=0.5, scalar2=None, op0=ALU.mult)
+
+        a_grp = const.tile([P, 2, V, 4], BF16, name="a_grp", align_bytes=64)
+        for g in range(2):
+            nc.vector.tensor_copy(out=a_grp[:, g], in_=a_raw[:, 4 * g:4 * g + 4, :].rearrange("q t w -> q w t"))
+        a_codes = const.tile([P, 2 * V], U32, name="a_codes", align_bytes=64)
+        a_scales = const.tile([P, 2 * V], U8, name="a_scales", align_bytes=64)
+        nc.vector.quantize_mx(out=a_codes[:].bitcast(FP8X4), scales=a_scales[:],
+                              in_=a_grp[:].rearrange("q g w t -> q (g w t)"))
+
+        gb_wide = const.tile([P, O, 2], F32, name="gb_wide")
+        gamma_pm = const.tile([P, 2], F32, name="gamma_pm")
+        beta_f = const.tile([P, 1], F32, name="beta_f")
+        gb_box = {}
+
+        def spread_rows():
+            nc.vector.tensor_tensor(out=gb_wide[:], in0=gb_rows[:, 0:O].unsqueeze(2).to_broadcast([P, O, 2]),
+                                    in1=gb_rows[:, O:2 * O].unsqueeze(2).to_broadcast([P, O, 2]), op=ALU.add)
+
+        def spread_matmul():
+            gb_ps = psum.tile([P, 2], F32, name="gb_ps", tag="bank%d" % MISC_BANK)
+            gb_box[0] = gb_ps
+            nc.tensor.matmul(out=gb_ps[:], lhsT=gb_wide[:].rearrange("p o r -> p (o r)"), rhs=ident[:, 0:2],
+                             start=True, stop=True)
+
+        def spread_out():
+            gb_ps = gb_box[0]
+            nc.vector.tensor_copy(out=gamma_pm[:, 0:1], in_=gb_ps[:, 0:1])
+            nc.vector.tensor_scalar(out=gamma_pm[:, 1:2], in0=gb_ps[:, 0:1], scalar1=-1.0, scalar2=None, op0=ALU.mult)
+            nc.vector.tensor_copy(out=beta_f[:], in_=gb_ps[:, 1:2])
+
+        z_codes = [keep.tile([P, 2 * P], U32, name="z_codes%d" % t, align_bytes=64) for t in range(TILES)]
+        z_scales = [keep.tile([P, 2 * P], U8, name="z_scales%d" % t, align_bytes=64) for t in range(TILES)]
+        stats = const.tile([P, PAIRS, 6], F32, name="stats")
+        turned = {}
+        grouped = {}
+        y_ps = {}
+        bank_of = {}
+
+        idle_ps = psum.tile([P, P], F32, name="idle_ps", tag="bank%d" % MISC_BANK)
+
+        def transposes(t):
+            c, k = where[t]
+            if k == 0 and c < 3:
+                for n in range(3):
+                    nc.tensor.matmul(out=idle_ps[:], lhsT=ident[:], rhs=ident[:], start=True, stop=True)
+            words = z_raw[c][:].rearrange("p n s v -> p (n s v)").bitcast(F32)
+            bank = psum.tile([P, S, P], F32, name="turned%d" % t, tag="bank%d" % (t % T_BANKS))
+            for g in range(2):
+                for u in range(2):
+                    w0 = (2 * k + g) * 2 * P
+                    nc.tensor.transpose(bank[:, 2 * g + u, :], words[:, w0 + u:w0 + 2 * P:2], ident[:])
+            turned[t] = bank
+
+        def evacuate(t):
+            gt = gpool.tile([P, 2, P, 4], BF16, name="grouped%d" % t, tag="grouped", align_bytes=64)
+            nc.scalar.copy(out=gt[:].bitcast(F32), in_=turned[t][:].rearrange("q (g u) r -> q g r u", u=2))
+            grouped[t] = gt
+
+        def quantise(t):
+            nc.vector.quantize_mx(out=z_codes[t][:].bitcast(FP8X4), scales=z_scales[t][:],
+                                  in_=grouped[t][:].rearrange("q g r t -> q (g r t)"))
+
+        def multiply(t, bank):
+            j = t // 2
+            if t % 2 == 0:
+                y_ps[j] = psum.tile([P, 2 * V], F32, name="y_ps%d_%d" % (j, bank), tag="bank%d" % bank)
+                bank_of[j] = bank
+            c0 = (t % 2) * V
+            for g in range(2):
+                nc.tensor.matmul_mx(out=y_ps[j][:, c0:c0 + V],
+                                    lhsT=z_codes[t][:, g * P:(g + 1) * P].bitcast(FP8X4),
+                                    lhsT_scale=z_scales[t][:, g * P:(g + 1) * P],
+                                    rhs=a_codes[:, g * V:(g + 1) * V].bitcast(FP8X4),
+                                    rhs_scale=a_scales[:, g * V:(g + 1) * V],
+                                    start=(g == 0), stop=(g == 1))
+
+        groups = [list(range(t0, min(t0 + GROUP, TILES))) for t0 in range(0, TILES, GROUP)]
+        n_groups = len(groups)
+        counted = 0
+        for i in range(n_groups + 1):
+            now = groups[i] if i < n_groups else []
+            before = groups[i - 1] if i > 0 else []
+            for t in now:
+                transposes(t)
+            for t in before:
+                multiply(t, T_BANKS + (t // 2) % Y_BANKS)
+            if i == n_groups // 2:
+                spread_matmul()
+            for t in now:
+                evacuate(t)
+            full = (before[-1] + 1) // 2 if before else 0
+            todo = list(now)
+            while todo or counted < full:
+                for t in todo[:2]:
+                    quantise(t)
+                todo = todo[2:]
+                if counted < full:
+                    nc.vector.bn_stats(out=stats[:, counted, :], in_=y_ps[counted][:])
+                    counted += 1
+            if i == n_groups // 2 - 1:
+                spread_rows()
+            if i == n_groups // 2:
+                spread_out()
+
+        mom = const.tile([P, 2], F32, name="mom")
+        nc.vector.bn_aggr(out=mom[:], in_=stats[:].rearrange("p j k -> p (j k)"))
+        nc.vector.scalar_tensor_tensor(out=mom[:, 1:2], in0=mom[:, 0:1], scalar=mom[:, 0:1], in1=mom[:, 1:2],
+                                       op0=ALU.mult, op1=ALU.add)
+        mom_ps = psum.tile([P, 2], F32, name="mom_ps", tag="bank%d" % MISC_BANK)
+        nc.tensor.matmul(out=mom_ps[:], lhsT=pair_avg[:].rearrange("p o r -> p (o r)"), rhs=mom[:],
+                         start=True, stop=True)
+
+        order = list(range(PAIRS - 4, PAIRS)) + list(range(PAIRS - 4))
+        again = [j for j in order if j < PAIRS - Y_BANKS]
+        free = list(range(T_BANKS))
+        done = [0]
+
+        def refill():
+            while free and done[0] < len(again):
+                j = again[done[0]]
+                bank = free[0]
+                free[:] = free[1:]
+                multiply(2 * j, bank)
+                multiply(2 * j + 1, bank)
+                done[0] += 1
+
+        refill()
+
+        negvar = const.tile([P, 1], F32, name="negvar")
+        nc.vector.tensor_scalar(out=negvar[:], in0=mom_ps[:, 0:1], scalar1=mom_ps[:, 0:1], scalar2=mom_ps[:, 1:2],
+                                op0=ALU.mult, op1=ALU.subtract)
+        std = const.tile([P, 1], F32, name="std")
+        nc.scalar.activation(out=std[:], in_=negvar[:], func=ACT.Sqrt, bias=eps_t[:, 0:1], scale=-1.0)
+        rstd = const.tile([P, 1], F32, name="rstd")
+        nc.vector.reciprocal(out=rstd[:], in_=std[:])
+        scale_pm = const.tile([P, 2], F32, name="scale_pm")
+        nc.vector.tensor_scalar(out=scale_pm[:], in0=gamma_pm[:], scalar1=rstd[:, 0:1], scalar2=None, op0=ALU.mult)
+        shift = const.tile([P, 1], F32, name="shift")
+        nc.vector.scalar_tensor_tensor(out=shift[:], in0=mom_ps[:, 0:1], scalar=scale_pm[:, 1:2], in1=beta_f[:],
+                                       op0=ALU.mult, op1=ALU.add)
+
+        res = {}
+        for j in order:
+            b = j // 4
+            c0 = (j % 4) * 2 * V
+            h = j % 2
+            if h == 0:
+                res[j // 2] = rpool.tile([P, 4 * V], F32, name="res%d" % (j // 2), tag="res")
+            part = res[j // 2][:, h * 2 * V:(h + 1) * 2 * V]
+            nc.vector.scalar_tensor_tensor(out=part, in0=y_ps[j][:], scalar=scale_pm[:, 0:1],
+                                           in1=x_sb[b][:, c0:c0 + 2 * V], op0=ALU.mult, op1=ALU.add)
+            nc.scalar.activation(out=part, in_=part, func=ACT.Relu, bias=shift[:, 0:1], scale=1.0)
+            if h == 1:
+                nc.sync.dma_start(out=ov[b, :, c0 - 2 * V:c0 + 2 * V], in_=res[j // 2][:])
+            free.append(bank_of[j])
+            refill()

@@ -10,60 +10,59 @@ U32 = mybir.dt.uint32
 U8 = mybir.dt.uint8
 ALU = mybir.AluOpType
 ACT = mybir.ActivationFunctionType
+AX = mybir.AxisListType
 
 S, B, O, T, V = 4, 4, 64, 16, 256
 P = 128
 EPS = 1e-5
 FLOPS = 2 * B * O * T * S * V * V
 
-TILES = B * O * T // P
-PAIRS = TILES // 2
-GROUP = 4
-T_BANKS = GROUP
-Y_BANKS = 7 - GROUP
-MISC_BANK = 7
-PIN = True
+OG = P // T
+G = O // OG
+TILES = G * B
+T_BANKS = 4
+LEAD = 6
 
 
 def tile_dggcn_sparse_assemble_pa_kernel(tc, z, A, x, gamma, beta, out):
     nc = tc.nc
     with ExitStack() as ctx:
-        if PIN:
-            ctx.enter_context(tc.manual_schedule())
+        ctx.enter_context(tc.manual_schedule())
         const = ctx.enter_context(tc.tile_pool(name="const", bufs=1))
         keep = ctx.enter_context(tc.tile_pool(name="keep", bufs=1))
         gpool = ctx.enter_context(tc.tile_pool(name="gpool", bufs=8))
-        rpool = ctx.enter_context(tc.tile_pool(name="rpool", bufs=4))
+        small = ctx.enter_context(tc.tile_pool(name="small", bufs=4))
         psum = ctx.enter_context(tc.psum_pool(name="psum", bufs=1))
 
-        zv = z.rearrange("s b o (th tl) v -> b s (o th) tl v", th=2)
-        xv = x.rearrange("b c (th tl) v -> b (c th) (tl v)", th=2)
-        ov = out.rearrange("b c (th tl) v -> b (c th) (tl v)", th=2)
+        zv = z.rearrange("s b (c o) t v -> c b (o t) s v", o=OG)
+        xv = x.rearrange("b (c o) t v -> c (o t) b v", o=OG)
+        ov = out.rearrange("b (c o) t v -> c (o t) b v", o=OG)
         av = A.rearrange("s v w -> (s v) w").rearrange("(g q t) w -> q g (t w)", q=P, t=4)
 
         gb_rows = const.tile([P, 2 * O], BF16, name="gb_rows")
         nc.vector.memset(gb_rows[:], 0.0)
         nc.scalar.dma_start(out=gb_rows[0:1, 0:O], in_=gamma.rearrange("(u o) -> u o", u=1))
-        nc.scalar.dma_start(out=gb_rows[1:2, O:2 * O], in_=beta.rearrange("(u o) -> u o", u=1))
+        nc.scalar.dma_start(out=gb_rows[0:1, O:2 * O], in_=beta.rearrange("(u o) -> u o", u=1))
 
-        chunks = [2, 2] + [4] * (TILES // 4 - 1)
-        z_raw = [keep.tile([P, n, S, V], BF16, name="z_raw%d" % c) for c, n in enumerate(chunks)]
-        where = [(c, k) for c, n in enumerate(chunks) for k in range(n)]
+        z_raw = [keep.tile([P, B, S, V], BF16, name="z_raw%d" % c) for c in range(G)]
+        x_sb = [keep.tile([P, B, V], BF16, name="x_sb%d" % c) for c in range(G)]
+        res = [keep.tile([P, B, V], F32, name="res%d" % c) for c in range(G)]
         a_raw = const.tile([P, 2 * S, V], BF16, name="a_raw")
-        x_sb = [keep.tile([P, 8 * V], BF16, name="x_sb%d" % b) for b in range(B)]
 
-        def load_z(c):
-            t0 = sum(chunks[:c])
-            tl = t0 % 8
-            for s in range(S):
-                nc.sync.dma_start(out=z_raw[c][:, :, s, :], in_=zv[t0 // 8, s, :, tl:tl + chunks[c], :])
+        def load_z(c, b):
+            nc.sync.dma_start(out=z_raw[c][:, b], in_=zv[c, b])
 
-        load_z(0)
+        def load_x(c):
+            nc.sync.dma_start(out=x_sb[c][:], in_=xv[c])
+
+        load_z(0, 0)
         nc.sync.dma_start(out=a_raw[:].rearrange("q (g t) w -> q g (t w)", t=4), in_=av)
-        for c in range(1, len(chunks)):
-            load_z(c)
-        for b in (3, 0, 1, 2):
-            nc.sync.dma_start(out=x_sb[b][:], in_=xv[b])
+        for b in range(1, B):
+            load_z(0, b)
+        for c in range(1, 5):
+            for b in range(B):
+                load_z(c, b)
+            load_x(c - 1)
 
         ident = const.tile([P, P], F32, name="ident")
         make_identity(nc, ident[:])
@@ -72,166 +71,213 @@ def tile_dggcn_sparse_assemble_pa_kernel(tc, z, A, x, gamma, beta, out):
         warm = const.tile([P, 1], F32, name="warm")
         nc.scalar.activation(out=warm[:], in_=one[:], func=ACT.Sqrt)
         eps_t = const.tile([P, 1], F32, name="eps_t")
-        nc.vector.memset(eps_t[:], EPS)
-        idv = ident[:].rearrange("p (o r) -> p o r", r=2)
-        half = const.tile([P, O], F32, name="half")
-        nc.vector.tensor_tensor(out=half[:], in0=idv[:, :, 0], in1=idv[:, :, 1], op=ALU.add)
-        pair_avg = const.tile([P, O, 2], F32, name="pair_avg")
-        nc.vector.tensor_scalar(out=pair_avg[:], in0=half[:].unsqueeze(2).to_broadcast([P, O, 2]),
-                                scalar1=0.5, scalar2=None, op0=ALU.mult)
+        nc.vector.tensor_scalar(out=eps_t[:], in0=one[:], scalar1=EPS, scalar2=None, op0=ALU.mult)
+        ones = const.tile([P, P], BF16, name="ones")
+        nc.vector.memset(ones[:], 1.0)
+        mask = const.tile([P, OG], F32, name="mask")
+        nc.vector.tensor_reduce(out=mask[:], in_=ident[:].rearrange("p (o t) -> p o t", t=T), op=ALU.add, axis=AX.X)
+        avg = const.tile([P, OG, T], F32, name="avg")
+        nc.vector.tensor_scalar(out=avg[:], in0=mask[:].unsqueeze(2).to_broadcast([P, OG, T]),
+                                scalar1=1.0 / T, scalar2=None, op0=ALU.mult)
 
         a_grp = const.tile([P, 2, V, 4], BF16, name="a_grp", align_bytes=64)
-        for g in range(2):
-            nc.vector.tensor_copy(out=a_grp[:, g], in_=a_raw[:, 4 * g:4 * g + 4, :].rearrange("q t w -> q w t"))
         a_codes = const.tile([P, 2 * V], U32, name="a_codes", align_bytes=64)
         a_scales = const.tile([P, 2 * V], U8, name="a_scales", align_bytes=64)
-        nc.vector.quantize_mx(out=a_codes[:].bitcast(FP8X4), scales=a_scales[:],
-                              in_=a_grp[:].rearrange("q g w t -> q (g w t)"))
 
-        gb_wide = const.tile([P, O, 2], F32, name="gb_wide")
-        gamma_pm = const.tile([P, 2], F32, name="gamma_pm")
-        beta_f = const.tile([P, 1], F32, name="beta_f")
+        def prepare_a():
+            for g in range(2):
+                nc.vector.tensor_copy(out=a_grp[:, g], in_=a_raw[:, 4 * g:4 * g + 4, :].rearrange("q t w -> q w t"))
+            nc.vector.quantize_mx(out=a_codes[:].bitcast(FP8X4), scales=a_scales[:],
+                                  in_=a_grp[:].rearrange("q g w t -> q (g w t)"))
+
+        banks = [0]
+
+        def next_bank():
+            banks[0] += 1
+            return "bank%d" % ((banks[0] - 1) % T_BANKS)
+
         gb_box = {}
-
-        def spread_rows():
-            nc.vector.tensor_tensor(out=gb_wide[:], in0=gb_rows[:, 0:O].unsqueeze(2).to_broadcast([P, O, 2]),
-                                    in1=gb_rows[:, O:2 * O].unsqueeze(2).to_broadcast([P, O, 2]), op=ALU.add)
+        gb_sel = const.tile([P, 2 * G, OG], F32, name="gb_sel")
+        gb_pm = const.tile([P, 2 * G], F32, name="gb_pm")
+        gamma2 = const.tile([P, G, 2], F32, name="gamma2")
 
         def spread_matmul():
-            gb_ps = psum.tile([P, 2], F32, name="gb_ps", tag="bank%d" % MISC_BANK)
+            gb_ps = psum.tile([P, 2 * O], F32, name="gb_ps", tag=next_bank())
             gb_box[0] = gb_ps
-            nc.tensor.matmul(out=gb_ps[:], lhsT=gb_wide[:].rearrange("p o r -> p (o r)"), rhs=ident[:, 0:2],
-                             start=True, stop=True)
+            nc.tensor.matmul(out=gb_ps[:], lhsT=ones[:], rhs=gb_rows[:], start=True, stop=True)
 
         def spread_out():
             gb_ps = gb_box[0]
-            nc.vector.tensor_copy(out=gamma_pm[:, 0:1], in_=gb_ps[:, 0:1])
-            nc.vector.tensor_scalar(out=gamma_pm[:, 1:2], in0=gb_ps[:, 0:1], scalar1=-1.0, scalar2=None, op0=ALU.mult)
-            nc.vector.tensor_copy(out=beta_f[:], in_=gb_ps[:, 1:2])
+            nc.vector.tensor_tensor(out=gb_sel[:], in0=gb_ps[:].rearrange("p (c o) -> p c o", o=OG),
+                                    in1=mask[:].unsqueeze(1).to_broadcast([P, 2 * G, OG]), op=ALU.mult)
+            nc.vector.tensor_reduce(out=gb_pm[:], in_=gb_sel[:], op=ALU.add, axis=AX.X)
+            nc.gpsimd.tensor_copy(out=gamma2[:, :, 0], in_=gb_pm[:, 0:G])
+            nc.gpsimd.tensor_scalar(out=gamma2[:, :, 1], in0=gb_pm[:, 0:G], scalar1=-1.0, scalar2=None, op0=ALU.mult)
 
-        z_codes = [keep.tile([P, 2 * P], U32, name="z_codes%d" % t, align_bytes=64) for t in range(TILES)]
-        z_scales = [keep.tile([P, 2 * P], U8, name="z_scales%d" % t, align_bytes=64) for t in range(TILES)]
-        stats = const.tile([P, PAIRS, 6], F32, name="stats")
-        turned = {}
-        grouped = {}
-        y_ps = {}
-        bank_of = {}
+        z_codes = [keep.tile([P, 2 * P], U32, name="z_codes%d" % n, align_bytes=64) for n in range(TILES)]
+        z_scales = [keep.tile([P, 2 * P], U8, name="z_scales%d" % n, align_bytes=64) for n in range(TILES)]
+        stats = [const.tile([P, 2, 6], F32, name="stats%d" % c) for c in range(G)]
+        turned, grouped, y_ps, mom, mom_ps = {}, {}, {}, {}, {}
+        negvar, std, rstd, scale_pm, shift = {}, {}, {}, {}, {}
 
-        idle_ps = psum.tile([P, P], F32, name="idle_ps", tag="bank%d" % MISC_BANK)
-
-        def transposes(t):
-            c, k = where[t]
-            if k == 0 and c < 3:
-                for n in range(3):
-                    nc.tensor.matmul(out=idle_ps[:], lhsT=ident[:], rhs=ident[:], start=True, stop=True)
-            words = z_raw[c][:].rearrange("p n s v -> p (n s v)").bitcast(F32)
-            bank = psum.tile([P, S, P], F32, name="turned%d" % t, tag="bank%d" % (t % T_BANKS))
+        def transposes(n):
+            words = z_raw[n // B][:, n % B].rearrange("p s v -> p (s v)").bitcast(F32)
+            bank = psum.tile([P, 4, P], F32, name="turned%d" % n, tag=next_bank())
             for g in range(2):
                 for u in range(2):
-                    w0 = (2 * k + g) * 2 * P
-                    nc.tensor.transpose(bank[:, 2 * g + u, :], words[:, w0 + u:w0 + 2 * P:2], ident[:])
-            turned[t] = bank
+                    nc.tensor.transpose(bank[:, 2 * g + u, :], words[:, 2 * P * g + u:2 * P * (g + 1):2], ident[:])
+            turned[n] = bank
 
-        def evacuate(t):
-            gt = gpool.tile([P, 2, P, 4], BF16, name="grouped%d" % t, tag="grouped", align_bytes=64)
-            nc.scalar.copy(out=gt[:].bitcast(F32), in_=turned[t][:].rearrange("q (g u) r -> q g r u", u=2))
-            grouped[t] = gt
+        def evacuate(n):
+            gt = gpool.tile([P, 2, P, 4], BF16, name="grouped%d" % n, tag="grouped", align_bytes=64)
+            nc.scalar.copy(out=gt[:].bitcast(F32), in_=turned[n][:].rearrange("q (g u) r -> q g r u", u=2))
+            grouped[n] = gt
 
-        def quantise(t):
-            nc.vector.quantize_mx(out=z_codes[t][:].bitcast(FP8X4), scales=z_scales[t][:],
-                                  in_=grouped[t][:].rearrange("q g r t -> q (g r t)"))
+        def quantise(n):
+            nc.vector.quantize_mx(out=z_codes[n][:].bitcast(FP8X4), scales=z_scales[n][:],
+                                  in_=grouped[n][:].rearrange("q g r t -> q (g r t)"))
 
-        def multiply(t, bank):
-            j = t // 2
-            if t % 2 == 0:
-                y_ps[j] = psum.tile([P, 2 * V], F32, name="y_ps%d_%d" % (j, bank), tag="bank%d" % bank)
-                bank_of[j] = bank
-            c0 = (t % 2) * V
+        def multiply(c, b):
+            n = c * B + b
+            j = b // 2
+            if b % 2 == 0:
+                y_ps[c, j] = psum.tile([P, 2 * V], F32, name="y_ps%d_%d" % (c, j), tag="bank%d" % (T_BANKS + (c % 2) * 2 + j))
+            c0 = (b % 2) * V
             for g in range(2):
-                nc.tensor.matmul_mx(out=y_ps[j][:, c0:c0 + V],
-                                    lhsT=z_codes[t][:, g * P:(g + 1) * P].bitcast(FP8X4),
-                                    lhsT_scale=z_scales[t][:, g * P:(g + 1) * P],
+                nc.tensor.matmul_mx(out=y_ps[c, j][:, c0:c0 + V],
+                                    lhsT=z_codes[n][:, g * P:(g + 1) * P].bitcast(FP8X4),
+                                    lhsT_scale=z_scales[n][:, g * P:(g + 1) * P],
                                     rhs=a_codes[:, g * V:(g + 1) * V].bitcast(FP8X4),
                                     rhs_scale=a_scales[:, g * V:(g + 1) * V],
                                     start=(g == 0), stop=(g == 1))
 
-        groups = [list(range(t0, min(t0 + GROUP, TILES))) for t0 in range(0, TILES, GROUP)]
-        n_groups = len(groups)
-        counted = 0
-        for i in range(n_groups + 1):
-            now = groups[i] if i < n_groups else []
-            before = groups[i - 1] if i > 0 else []
-            for t in now:
-                transposes(t)
-            for t in before:
-                multiply(t, T_BANKS + (t // 2) % Y_BANKS)
-            if i == n_groups // 2:
-                spread_matmul()
-            for t in now:
-                evacuate(t)
-            full = (before[-1] + 1) // 2 if before else 0
-            todo = list(now)
-            while todo or counted < full:
-                for t in todo[:2]:
-                    quantise(t)
-                todo = todo[2:]
-                if counted < full:
-                    nc.vector.bn_stats(out=stats[:, counted, :], in_=y_ps[counted][:])
-                    counted += 1
-            if i == n_groups // 2 - 1:
-                spread_rows()
-            if i == n_groups // 2:
-                spread_out()
+        def measure(c, j):
+            nc.vector.bn_stats(out=stats[c][:, j, :], in_=y_ps[c, j][:])
 
-        mom = const.tile([P, 2], F32, name="mom")
-        nc.vector.bn_aggr(out=mom[:], in_=stats[:].rearrange("p j k -> p (j k)"))
-        nc.vector.scalar_tensor_tensor(out=mom[:, 1:2], in0=mom[:, 0:1], scalar=mom[:, 0:1], in1=mom[:, 1:2],
-                                       op0=ALU.mult, op1=ALU.add)
-        mom_ps = psum.tile([P, 2], F32, name="mom_ps", tag="bank%d" % MISC_BANK)
-        nc.tensor.matmul(out=mom_ps[:], lhsT=pair_avg[:].rearrange("p o r -> p (o r)"), rhs=mom[:],
-                         start=True, stop=True)
+        def aggregate(c):
+            m = small.tile([P, 2], F32, name="mom%d" % c, tag="mom")
+            mom[c] = m
+            nc.vector.bn_aggr(out=m[:], in_=stats[c][:].rearrange("p j k -> p (j k)"))
 
-        order = list(range(PAIRS - 4, PAIRS)) + list(range(PAIRS - 4))
-        again = [j for j in order if j < PAIRS - Y_BANKS]
-        free = list(range(T_BANKS))
-        done = [0]
+        def second_moment(c):
+            m = mom[c]
+            nc.vector.scalar_tensor_tensor(out=m[:, 1:2], in0=m[:, 0:1], scalar=m[:, 0:1], in1=m[:, 1:2],
+                                           op0=ALU.mult, op1=ALU.add)
 
-        def refill():
-            while free and done[0] < len(again):
-                j = again[done[0]]
-                bank = free[0]
-                free[:] = free[1:]
-                multiply(2 * j, bank)
-                multiply(2 * j + 1, bank)
-                done[0] += 1
+        def average(c):
+            mp = psum.tile([P, 2], F32, name="mom_ps%d" % c, tag=next_bank())
+            nc.tensor.matmul(out=mp[:], lhsT=avg[:].rearrange("p o t -> p (o t)"), rhs=mom[c][:], start=True, stop=True)
+            mom_ps[c] = mp
 
-        refill()
+        def minus_variance(c):
+            nv = small.tile([P, 1], F32, name="negvar%d" % c, tag="negvar")
+            nc.vector.tensor_scalar(out=nv[:], in0=mom_ps[c][:, 0:1], scalar1=mom_ps[c][:, 0:1],
+                                    scalar2=mom_ps[c][:, 1:2], op0=ALU.mult, op1=ALU.subtract)
+            negvar[c] = nv
 
-        negvar = const.tile([P, 1], F32, name="negvar")
-        nc.vector.tensor_scalar(out=negvar[:], in0=mom_ps[:, 0:1], scalar1=mom_ps[:, 0:1], scalar2=mom_ps[:, 1:2],
-                                op0=ALU.mult, op1=ALU.subtract)
-        std = const.tile([P, 1], F32, name="std")
-        nc.scalar.activation(out=std[:], in_=negvar[:], func=ACT.Sqrt, bias=eps_t[:, 0:1], scale=-1.0)
-        rstd = const.tile([P, 1], F32, name="rstd")
-        nc.vector.reciprocal(out=rstd[:], in_=std[:])
-        scale_pm = const.tile([P, 2], F32, name="scale_pm")
-        nc.vector.tensor_scalar(out=scale_pm[:], in0=gamma_pm[:], scalar1=rstd[:, 0:1], scalar2=None, op0=ALU.mult)
-        shift = const.tile([P, 1], F32, name="shift")
-        nc.vector.scalar_tensor_tensor(out=shift[:], in0=mom_ps[:, 0:1], scalar=scale_pm[:, 1:2], in1=beta_f[:],
-                                       op0=ALU.mult, op1=ALU.add)
+        def deviation(c):
+            sd = small.tile([P, 1], F32, name="std%d" % c, tag="std")
+            nc.scalar.activation(out=sd[:], in_=negvar[c][:], func=ACT.Sqrt, bias=eps_t[:, 0:1], scale=-1.0)
+            std[c] = sd
 
-        res = {}
-        for j in order:
-            b = j // 4
-            c0 = (j % 4) * 2 * V
-            h = j % 2
+        def invert(c):
+            rs = small.tile([P, 1], F32, name="rstd%d" % c, tag="rstd")
+            nc.vector.reciprocal(out=rs[:], in_=std[c][:])
+            rstd[c] = rs
+
+        def scales(c):
+            sc = small.tile([P, 2], F32, name="scale_pm%d" % c, tag="scale_pm")
+            nc.gpsimd.tensor_scalar(out=sc[:], in0=gamma2[:, c, :], scalar1=rstd[c][:, 0:1], scalar2=None, op0=ALU.mult)
+            scale_pm[c] = sc
+
+        def shifts(c):
+            sh = small.tile([P, 1], F32, name="shift%d" % c, tag="shift")
+            nc.scalar.activation(out=sh[:], in_=mom_ps[c][:, 0:1], func=ACT.Identity, bias=gb_pm[:, G + c:G + c + 1],
+                                 scale=scale_pm[c][:, 1:2])
+            shift[c] = sh
+
+        def normalise(c, j):
+            nc.vector.scalar_tensor_tensor(out=res[c][:, 2 * j:2 * j + 2, :].rearrange("p b v -> p (b v)"),
+                                           in0=y_ps[c, j][:], scalar=scale_pm[c][:, 0:1],
+                                           in1=x_sb[c][:, 2 * j:2 * j + 2, :].rearrange("p b v -> p (b v)"),
+                                           op0=ALU.mult, op1=ALU.add)
+
+        def rectify(c, j):
+            part = res[c][:, 2 * j:2 * j + 2, :]
+            flat = part.rearrange("p b v -> p (b v)")
+            nc.scalar.activation(out=flat, in_=flat, func=ACT.Relu, bias=shift[c][:, 0:1], scale=1.0)
+            nc.sync.dma_start(out=ov[c][:, 2 * j:2 * j + 2, :], in_=part)
+
+        turned_to = [0]
+        evacuated_to = [0]
+
+        def turn(upto):
+            while turned_to[0] < min(upto, TILES):
+                transposes(turned_to[0])
+                turned_to[0] += 1
+
+        def empty(upto):
+            while evacuated_to[0] < min(upto, TILES):
+                evacuate(evacuated_to[0])
+                evacuated_to[0] += 1
+
+        turn(1)
+        empty(1)
+        for h in range(G + 1):
+            g = h - 1
             if h == 0:
-                res[j // 2] = rpool.tile([P, 4 * V], F32, name="res%d" % (j // 2), tag="res")
-            part = res[j // 2][:, h * 2 * V:(h + 1) * 2 * V]
-            nc.vector.scalar_tensor_tensor(out=part, in0=y_ps[j][:], scalar=scale_pm[:, 0:1],
-                                           in1=x_sb[b][:, c0:c0 + 2 * V], op0=ALU.mult, op1=ALU.add)
-            nc.scalar.activation(out=part, in_=part, func=ACT.Relu, bias=shift[:, 0:1], scale=1.0)
-            if h == 1:
-                nc.sync.dma_start(out=ov[b, :, c0 - 2 * V:c0 + 2 * V], in_=res[j // 2][:])
-            free.append(bank_of[j])
-            refill()
+                for n in range(1, B):
+                    turn(n + 1)
+                    empty(n + 1)
+                quantise(0)
+                prepare_a()
+                for n in range(1, B):
+                    quantise(n)
+            else:
+                average(g)
+                empty(4 * h + 5)
+                if g > 0:
+                    rectify(g - 1, 1)
+                if h < G:
+                    for b in range(3):
+                        quantise(4 * h + b)
+                minus_variance(g)
+                deviation(g)
+                if h < G:
+                    quantise(4 * h + 3)
+                if h + 4 < G:
+                    for b in range(B):
+                        load_z(h + 4, b)
+                if h + 3 < G:
+                    load_x(h + 3)
+            if h < G:
+                for b in range(B):
+                    multiply(h, b)
+                measure(h, 0)
+            if h > 0:
+                empty(4 * h + 6)
+                invert(g)
+                scales(g)
+            if h < G:
+                measure(h, 1)
+            if h == 0:
+                spread_matmul()
+                spread_out()
+            turn(4 * h + LEAD + 1)
+            turn(4 * h + LEAD + 2)
+            empty(4 * h + 7)
+            if h > 0:
+                shifts(g)
+            turn(4 * h + LEAD + 3)
+            empty(4 * h + 8)
+            turn(4 * h + LEAD + 4)
+            if h > 0:
+                normalise(g, 0)
+            if h < G:
+                aggregate(h)
+            if h > 0:
+                normalise(g, 1)
+                rectify(g, 0)
+            if h < G:
+                second_moment(h)
+        rectify(G - 1, 1)

@@ -59,10 +59,11 @@ def tile_dggcn_sparse_assemble_pa_kernel(tc, z, A, x, gamma, beta, out):
         nc.sync.dma_start(out=a_raw[:].rearrange("q (g t) w -> q g (t w)", t=4), in_=av)
         for b in range(1, B):
             load_z(0, b)
-        for c in range(1, 5):
+        for c in range(1, G):
             for b in range(B):
                 load_z(c, b)
             load_x(c - 1)
+        load_x(G - 1)
 
         ident = const.tile([P, P], F32, name="ident")
         make_identity(nc, ident[:])
@@ -245,11 +246,6 @@ def tile_dggcn_sparse_assemble_pa_kernel(tc, z, A, x, gamma, beta, out):
                 deviation(g)
                 if h < G:
                     quantise(4 * h + 3)
-                if h + 4 < G:
-                    for b in range(B):
-                        load_z(h + 4, b)
-                if h + 3 < G:
-                    load_x(h + 3)
             if h < G:
                 for b in range(B):
                     multiply(h, b)

@@ -62,7 +62,9 @@ def tile_dggcn_sparse_assemble_pa_kernel(tc, z, A, x, gamma, beta, out):
         for c in range(1, G):
             for b in range(B):
                 load_z(c, b)
-            load_x(c - 1)
+            if c > 1:
+                load_x(c - 2)
+        load_x(G - 2)
         load_x(G - 1)
 
         ident = const.tile([P, P], F32, name="ident")
@@ -188,7 +190,8 @@ def tile_dggcn_sparse_assemble_pa_kernel(tc, z, A, x, gamma, beta, out):
 
         def scales(c):
             sc = small.tile([P, 2], F32, name="scale_pm%d" % c, tag="scale_pm")
-            nc.gpsimd.tensor_scalar(out=sc[:], in0=gamma2[:, c, :], scalar1=rstd[c][:, 0:1], scalar2=None, op0=ALU.mult)
+            engine = nc.gpsimd if c < G - 1 else nc.vector
+            engine.tensor_scalar(out=sc[:], in0=gamma2[:, c, :], scalar1=rstd[c][:, 0:1], scalar2=None, op0=ALU.mult)
             scale_pm[c] = sc
 
         def shifts(c):
@@ -224,7 +227,7 @@ def tile_dggcn_sparse_assemble_pa_kernel(tc, z, A, x, gamma, beta, out):
 
         turn(1)
         empty(1)
-        for h in range(G + 1):
+        for h in range(G):
             g = h - 1
             if h == 0:
                 for n in range(1, B):
@@ -239,23 +242,19 @@ def tile_dggcn_sparse_assemble_pa_kernel(tc, z, A, x, gamma, beta, out):
                 empty(4 * h + 5)
                 if g > 0:
                     rectify(g - 1, 1)
-                if h < G:
-                    for b in range(3):
-                        quantise(4 * h + b)
+                for b in range(3):
+                    quantise(4 * h + b)
                 minus_variance(g)
                 deviation(g)
-                if h < G:
-                    quantise(4 * h + 3)
-            if h < G:
-                for b in range(B):
-                    multiply(h, b)
-                measure(h, 0)
+                quantise(4 * h + 3)
+            for b in range(B):
+                multiply(h, b)
+            measure(h, 0)
             if h > 0:
                 empty(4 * h + 6)
                 invert(g)
                 scales(g)
-            if h < G:
-                measure(h, 1)
+            measure(h, 1)
             if h == 0:
                 spread_matmul()
                 spread_out()
@@ -267,13 +266,28 @@ def tile_dggcn_sparse_assemble_pa_kernel(tc, z, A, x, gamma, beta, out):
             turn(4 * h + LEAD + 3)
             empty(4 * h + 8)
             turn(4 * h + LEAD + 4)
-            if h > 0:
-                normalise(g, 0)
-            if h < G:
+            if h < G - 1:
+                if h > 0:
+                    normalise(g, 0)
                 aggregate(h)
-            if h > 0:
-                normalise(g, 1)
-                rectify(g, 0)
-            if h < G:
+                if h > 0:
+                    normalise(g, 1)
+                    rectify(g, 0)
                 second_moment(h)
-        rectify(G - 1, 1)
+
+        g = G - 1
+        aggregate(g)
+        second_moment(g)
+        average(g)
+        normalise(g - 1, 0)
+        minus_variance(g)
+        deviation(g)
+        normalise(g - 1, 1)
+        rectify(g - 1, 0)
+        rectify(g - 1, 1)
+        invert(g)
+        scales(g)
+        shifts(g)
+        for j in range(2):
+            normalise(g, j)
+            rectify(g, j)

@@ -17,8 +17,12 @@ P = 128
 EPS = 1e-5
 FLOPS = 2 * B * O * T * S * V * V
 
-OG = P // T
+OG = 8
 G = O // OG
+BL = 2
+BH = B // BL
+TL = OG * T * BL // P
+TH = T // TL
 TILES = G * B
 T_BANKS = 4
 LEAD = 6
@@ -34,31 +38,33 @@ def tile_dggcn_sparse_assemble_pa_kernel(tc, z, A, x, gamma, beta, out):
         small = ctx.enter_context(tc.tile_pool(name="small", bufs=4))
         psum = ctx.enter_context(tc.psum_pool(name="psum", bufs=1))
 
-        zv = z.rearrange("s b (c o) t v -> c b (o t) s v", o=OG)
-        xv = x.rearrange("b (c o) t v -> c (o t) b v", o=OG)
-        ov = out.rearrange("b (c o) t v -> c (o t) b v", o=OG)
+        zv = z.rearrange("s (bh bl) (c o) (th k) v -> c bh bl k (o th) s v", bl=BL, o=OG, k=TL)
+        xv = x.rearrange("(bh bl) (c o) (th k) v -> c bl (o th) bh (k v)", bl=BL, o=OG, k=TL)
+        ov = out.rearrange("(bh bl) (c o) (th k) v -> c bl (o th) bh (k v)", bl=BL, o=OG, k=TL)
         av = A.rearrange("s v w -> (s v) w").rearrange("(g q t) w -> q g (t w)", q=P, t=4)
 
         gb_rows = const.tile([P, 2 * O], BF16, name="gb_rows")
         nc.vector.memset(gb_rows[:], 0.0)
-        nc.scalar.dma_start(out=gb_rows[0:1, 0:O], in_=gamma.rearrange("(u o) -> u o", u=1))
-        nc.scalar.dma_start(out=gb_rows[0:1, O:2 * O], in_=beta.rearrange("(u o) -> u o", u=1))
 
-        z_raw = [keep.tile([P, B, S, V], BF16, name="z_raw%d" % c) for c in range(G)]
-        x_sb = [keep.tile([P, B, V], BF16, name="x_sb%d" % c) for c in range(G)]
-        res = [keep.tile([P, B, V], F32, name="res%d" % c) for c in range(G)]
+        z_raw = [keep.tile([P, S, V], BF16, name="z_raw%d" % n) for n in range(TILES)]
+        x_sb = [keep.tile([P, BH, TL * V], BF16, name="x_sb%d" % c) for c in range(G)]
+        res = [keep.tile([P, BH, TL * V], F32, name="res%d" % c) for c in range(G)]
         a_raw = const.tile([P, 2 * S, V], BF16, name="a_raw")
 
         def load_z(c, b):
-            nc.sync.dma_start(out=z_raw[c][:, b], in_=zv[c, b])
+            for bl in range(BL):
+                nc.sync.dma_start(out=z_raw[c * B + b][bl::BL], in_=zv[c, b // TL, bl, b % TL])
 
         def load_x(c):
-            nc.sync.dma_start(out=x_sb[c][:], in_=xv[c])
+            for bl in range(BL):
+                nc.sync.dma_start(out=x_sb[c][bl::BL], in_=xv[c, bl])
 
         load_z(0, 0)
         nc.sync.dma_start(out=a_raw[:].rearrange("q (g t) w -> q g (t w)", t=4), in_=av)
         for b in range(1, B):
             load_z(0, b)
+        nc.sync.dma_start(out=gb_rows[0:1, 0:O], in_=gamma.rearrange("(u o) -> u o", u=1))
+        nc.sync.dma_start(out=gb_rows[0:1, O:2 * O], in_=beta.rearrange("(u o) -> u o", u=1))
         for c in range(1, G):
             for b in range(B):
                 load_z(c, b)
@@ -78,10 +84,10 @@ def tile_dggcn_sparse_assemble_pa_kernel(tc, z, A, x, gamma, beta, out):
         ones = const.tile([P, P], BF16, name="ones")
         nc.vector.memset(ones[:], 1.0)
         mask = const.tile([P, OG], F32, name="mask")
-        nc.vector.tensor_reduce(out=mask[:], in_=ident[:].rearrange("p (o t) -> p o t", t=T), op=ALU.add, axis=AX.X)
-        avg = const.tile([P, OG, T], F32, name="avg")
-        nc.vector.tensor_scalar(out=avg[:], in0=mask[:].unsqueeze(2).to_broadcast([P, OG, T]),
-                                scalar1=1.0 / T, scalar2=None, op0=ALU.mult)
+        nc.vector.tensor_reduce(out=mask[:], in_=ident[:].rearrange("p (o t) -> p o t", t=P // OG), op=ALU.add, axis=AX.X)
+        avg = const.tile([P, OG, P // OG], F32, name="avg")
+        nc.vector.tensor_scalar(out=avg[:], in0=mask[:].unsqueeze(2).to_broadcast([P, OG, P // OG]),
+                                scalar1=OG / P, scalar2=None, op0=ALU.mult)
 
         a_grp = const.tile([P, 2, V, 4], BF16, name="a_grp", align_bytes=64)
         a_codes = const.tile([P, 2 * V], U32, name="a_codes", align_bytes=64)
@@ -124,7 +130,7 @@ def tile_dggcn_sparse_assemble_pa_kernel(tc, z, A, x, gamma, beta, out):
         negvar, std, rstd, scale_pm, shift = {}, {}, {}, {}, {}
 
         def transposes(n):
-            words = z_raw[n // B][:, n % B].rearrange("p s v -> p (s v)").bitcast(F32)
+            words = z_raw[n][:].rearrange("p s v -> p (s v)").bitcast(F32)
             bank = psum.tile([P, 4, P], F32, name="turned%d" % n, tag=next_bank())
             for g in range(2):
                 for u in range(2):
@@ -201,16 +207,17 @@ def tile_dggcn_sparse_assemble_pa_kernel(tc, z, A, x, gamma, beta, out):
             shift[c] = sh
 
         def normalise(c, j):
-            nc.vector.scalar_tensor_tensor(out=res[c][:, 2 * j:2 * j + 2, :].rearrange("p b v -> p (b v)"),
-                                           in0=y_ps[c, j][:], scalar=scale_pm[c][:, 0:1],
-                                           in1=x_sb[c][:, 2 * j:2 * j + 2, :].rearrange("p b v -> p (b v)"),
-                                           op0=ALU.mult, op1=ALU.add)
+            nc.vector.scalar_tensor_tensor(out=res[c][:, j, :], in0=y_ps[c, j][:], scalar=scale_pm[c][:, 0:1],
+                                           in1=x_sb[c][:, j, :], op0=ALU.mult, op1=ALU.add)
 
         def rectify(c, j):
-            part = res[c][:, 2 * j:2 * j + 2, :]
-            flat = part.rearrange("p b v -> p (b v)")
-            nc.scalar.activation(out=flat, in_=flat, func=ACT.Relu, bias=shift[c][:, 0:1], scale=1.0)
-            nc.sync.dma_start(out=ov[c][:, 2 * j:2 * j + 2, :], in_=part)
+            part = res[c][:, j, :]
+            nc.scalar.activation(out=part, in_=part, func=ACT.Relu, bias=shift[c][:, 0:1], scale=1.0)
+            for bl in range(BL):
+                if c == G - 1:
+                    nc.sync.dma_start(out=ov[c, bl, :, j], in_=res[c][bl::BL, j, :])
+                elif j == BH - 1:
+                    nc.sync.dma_start(out=ov[c, bl], in_=res[c][bl::BL])
 
         turned_to = [0]
         evacuated_to = [0]

@@ -78,7 +78,7 @@ def tile_dggcn_sparse_assemble_pa_kernel(tc, z, A, x, gamma, beta, out):
         one = const.tile([P, 1], F32, name="one")
         nc.vector.memset(one[:], 1.0)
         warm = const.tile([P, 1], F32, name="warm")
-        nc.scalar.activation(out=warm[:], in_=one[:], func=ACT.Sqrt)
+        nc.scalar.activation(out=warm[:], in_=one[:], func=ACT.Abs_reciprocal_sqrt)
         eps_t = const.tile([P, 1], F32, name="eps_t")
         nc.vector.tensor_scalar(out=eps_t[:], in0=one[:], scalar1=EPS, scalar2=None, op0=ALU.mult)
         ones = const.tile([P, P], BF16, name="ones")
@@ -127,7 +127,7 @@ def tile_dggcn_sparse_assemble_pa_kernel(tc, z, A, x, gamma, beta, out):
         z_scales = [keep.tile([P, 2 * P], U8, name="z_scales%d" % n, align_bytes=64) for n in range(TILES)]
         stats = [const.tile([P, 2, 6], F32, name="stats%d" % c) for c in range(G)]
         turned, grouped, y_ps, mom, mom_ps = {}, {}, {}, {}, {}
-        negvar, std, rstd, scale_pm, shift = {}, {}, {}, {}, {}
+        negvar, rstd, scale_pm, shift = {}, {}, {}, {}
 
         def transposes(n):
             words = z_raw[n][:].rearrange("p s v -> p (s v)").bitcast(F32)
@@ -185,13 +185,8 @@ def tile_dggcn_sparse_assemble_pa_kernel(tc, z, A, x, gamma, beta, out):
             negvar[c] = nv
 
         def deviation(c):
-            sd = small.tile([P, 1], F32, name="std%d" % c, tag="std")
-            nc.scalar.activation(out=sd[:], in_=negvar[c][:], func=ACT.Sqrt, bias=eps_t[:, 0:1], scale=-1.0)
-            std[c] = sd
-
-        def invert(c):
             rs = small.tile([P, 1], F32, name="rstd%d" % c, tag="rstd")
-            nc.vector.reciprocal(out=rs[:], in_=std[c][:])
+            nc.scalar.activation(out=rs[:], in_=negvar[c][:], func=ACT.Abs_reciprocal_sqrt, bias=eps_t[:, 0:1], scale=-1.0)
             rstd[c] = rs
 
         def scales(c):
@@ -212,12 +207,21 @@ def tile_dggcn_sparse_assemble_pa_kernel(tc, z, A, x, gamma, beta, out):
 
         def rectify(c, j):
             part = res[c][:, j, :]
-            nc.scalar.activation(out=part, in_=part, func=ACT.Relu, bias=shift[c][:, 0:1], scale=1.0)
+            if c == G - 1 and j == BH - 1:
+                nc.vector.tensor_scalar(out=part, in0=part, scalar1=shift[c][:, 0:1], scalar2=0.0,
+                                        op0=ALU.add, op1=ALU.max)
+            else:
+                nc.scalar.activation(out=part, in_=part, func=ACT.Relu, bias=shift[c][:, 0:1], scale=1.0)
             for bl in range(BL):
-                if c == G - 1:
+                if c >= G - 2:
                     nc.sync.dma_start(out=ov[c, bl, :, j], in_=res[c][bl::BL, j, :])
                 elif j == BH - 1:
                     nc.sync.dma_start(out=ov[c, bl], in_=res[c][bl::BL])
+
+        def keep_warm():
+            idle_ps = psum.tile([P, P], F32, name="idle_ps", tag=next_bank())
+            for n in range(4):
+                nc.tensor.matmul(out=idle_ps[:], lhsT=ident[:], rhs=ident[:], start=True, stop=True)
 
         turned_to = [0]
         evacuated_to = [0]
@@ -237,7 +241,7 @@ def tile_dggcn_sparse_assemble_pa_kernel(tc, z, A, x, gamma, beta, out):
         for h in range(G):
             g = h - 1
             if h == 0:
-                for n in range(1, B):
+                for n in range(1, B + 1):
                     turn(n + 1)
                     empty(n + 1)
                 quantise(0)
@@ -245,21 +249,21 @@ def tile_dggcn_sparse_assemble_pa_kernel(tc, z, A, x, gamma, beta, out):
                 for n in range(1, B):
                     quantise(n)
             else:
+                if h == G - 1:
+                    keep_warm()
                 average(g)
                 empty(4 * h + 5)
-                if g > 0:
-                    rectify(g - 1, 1)
-                for b in range(3):
+                for b in range(B):
                     quantise(4 * h + b)
                 minus_variance(g)
                 deviation(g)
-                quantise(4 * h + 3)
+                if g > 0:
+                    rectify(g - 1, 1)
             for b in range(B):
                 multiply(h, b)
             measure(h, 0)
             if h > 0:
                 empty(4 * h + 6)
-                invert(g)
                 scales(g)
             measure(h, 1)
             if h == 0:
@@ -292,7 +296,6 @@ def tile_dggcn_sparse_assemble_pa_kernel(tc, z, A, x, gamma, beta, out):
         normalise(g - 1, 1)
         rectify(g - 1, 0)
         rectify(g - 1, 1)
-        invert(g)
         scales(g)
         shifts(g)
         for j in range(2):

from contextlib import ExitStack

import concourse.mybir as mybir
from concourse.masks import make_identity

FP8X4 = mybir.dt.float8_e4m3fn_x4
BF16 = mybir.dt.bfloat16
F32 = mybir.dt.float32
U32 = mybir.dt.uint32
U8 = mybir.dt.uint8
ALU = mybir.AluOpType
ACT = mybir.ActivationFunctionType
AX = mybir.AxisListType

S, B, O, T, V = 4, 4, 64, 16, 256
P = 128
EPS = 1e-5
FLOPS = 2 * B * O * T * S * V * V

OG = 8
G = O // OG
BL = 2
BH = B // BL
TL = OG * T * BL // P
TH = T // TL
TILES = G * B
T_BANKS = 4
LEAD = 6


def tile_dggcn_sparse_assemble_pa_kernel(tc, z, A, x, gamma, beta, out):
    nc = tc.nc
    with ExitStack() as ctx:
        ctx.enter_context(tc.manual_schedule())
        const = ctx.enter_context(tc.tile_pool(name="const", bufs=1))
        keep = ctx.enter_context(tc.tile_pool(name="keep", bufs=1))
        gpool = ctx.enter_context(tc.tile_pool(name="gpool", bufs=8))
        small = ctx.enter_context(tc.tile_pool(name="small", bufs=4))
        psum = ctx.enter_context(tc.psum_pool(name="psum", bufs=1))

        zv = z.rearrange("s (bh bl) (c o) (th k) v -> c bh bl k (o th) s v", bl=BL, o=OG, k=TL)
        xv = x.rearrange("(bh bl) (c o) (th k) v -> c bl (o th) bh (k v)", bl=BL, o=OG, k=TL)
        ov = out.rearrange("(bh bl) (c o) (th k) v -> c bl (o th) bh (k v)", bl=BL, o=OG, k=TL)
        av = A.rearrange("s v w -> (s v) w").rearrange("(g q t) w -> q g (t w)", q=P, t=4)

        gb_rows = const.tile([P, 2 * O], BF16, name="gb_rows")
        nc.vector.memset(gb_rows[:], 0.0)

        z_raw = [keep.tile([P, S, V], BF16, name="z_raw%d" % n) for n in range(TILES)]
        x_sb = [keep.tile([P, BH, TL * V], BF16, name="x_sb%d" % c) for c in range(G)]
        res = [keep.tile([P, BH, TL * V], F32, name="res%d" % c) for c in range(G)]
        a_raw = const.tile([P, 2 * S, V], BF16, name="a_raw")

        def load_z(c, b):
            for bl in range(BL):
                nc.sync.dma_start(out=z_raw[c * B + b][bl::BL], in_=zv[c, b // TL, bl, b % TL])

        def load_x(c):
            for bl in range(BL):
                nc.sync.dma_start(out=x_sb[c][bl::BL], in_=xv[c, bl])

        load_z(0, 0)
        nc.sync.dma_start(out=a_raw[:].rearrange("q (g t) w -> q g (t w)", t=4), in_=av)
        for b in range(1, B):
            load_z(0, b)
        nc.sync.dma_start(out=gb_rows[0:1, 0:O], in_=gamma.rearrange("(u o) -> u o", u=1))
        nc.sync.dma_start(out=gb_rows[0:1, O:2 * O], in_=beta.rearrange("(u o) -> u o", u=1))
        for c in range(1, G):
            for b in range(B):
                load_z(c, b)
            if c > 1:
                load_x(c - 2)
        load_x(G - 2)
        load_x(G - 1)

        ident = const.tile([P, P], F32, name="ident")
        make_identity(nc, ident[:])
        one = const.tile([P, 1], F32, name="one")
        nc.vector.memset(one[:], 1.0)
        warm = const.tile([P, 1], F32, name="warm")
        nc.scalar.activation(out=warm[:], in_=one[:], func=ACT.Abs_reciprocal_sqrt)
        eps_t = const.tile([P, 1], F32, name="eps_t")
        nc.vector.tensor_scalar(out=eps_t[:], in0=one[:], scalar1=EPS, scalar2=None, op0=ALU.mult)
        ones = const.tile([P, P], BF16, name="ones")
        nc.vector.memset(ones[:], 1.0)
        mask = const.tile([P, OG], F32, name="mask")
        nc.vector.tensor_reduce(out=mask[:], in_=ident[:].rearrange("p (o t) -> p o t", t=P // OG), op=ALU.add, axis=AX.X)
        avg = const.tile([P, OG, P // OG], F32, name="avg")
        nc.vector.tensor_scalar(out=avg[:], in0=mask[:].unsqueeze(2).to_broadcast([P, OG, P // OG]),
                                scalar1=OG / P, scalar2=None, op0=ALU.mult)

        a_grp = const.tile([P, 2, V, 4], BF16, name="a_grp", align_bytes=64)
        a_codes = const.tile([P, 2 * V], U32, name="a_codes", align_bytes=64)
        a_scales = const.tile([P, 2 * V], U8, name="a_scales", align_bytes=64)

        def prepare_a():
            for g in range(2):
                nc.vector.tensor_copy(out=a_grp[:, g], in_=a_raw[:, 4 * g:4 * g + 4, :].rearrange("q t w -> q w t"))
            nc.vector.quantize_mx(out=a_codes[:].bitcast(FP8X4), scales=a_scales[:],
                                  in_=a_grp[:].rearrange("q g w t -> q (g w t)"))

        banks = [0]

        def next_bank():
            banks[0] += 1
            return "bank%d" % ((banks[0] - 1) % T_BANKS)

        gb_box = {}
        gb_sel = const.tile([P, 2 * G, OG], F32, name="gb_sel")
        gb_pm = const.tile([P, 2 * G], F32, name="gb_pm")
        gamma2 = const.tile([P, G, 2], F32, name="gamma2")

        def spread_matmul():
            gb_ps = psum.tile([P, 2 * O], F32, name="gb_ps", tag=next_bank())
            gb_box[0] = gb_ps
            nc.tensor.matmul(out=gb_ps[:], lhsT=ones[:], rhs=gb_rows[:], start=True, stop=True)

        def spread_out():
            gb_ps = gb_box[0]
            nc.vector.tensor_tensor(out=gb_sel[:], in0=gb_ps[:].rearrange("p (c o) -> p c o", o=OG),
                                    in1=mask[:].unsqueeze(1).to_broadcast([P, 2 * G, OG]), op=ALU.mult)
            nc.vector.tensor_reduce(out=gb_pm[:], in_=gb_sel[:], op=ALU.add, axis=AX.X)
            nc.gpsimd.tensor_copy(out=gamma2[:, :, 0], in_=gb_pm[:, 0:G])
            nc.gpsimd.tensor_scalar(out=gamma2[:, :, 1], in0=gb_pm[:, 0:G], scalar1=-1.0, scalar2=None, op0=ALU.mult)

        z_codes = [keep.tile([P, 2 * P], U32, name="z_codes%d" % n, align_bytes=64) for n in range(TILES)]
        z_scales = [keep.tile([P, 2 * P], U8, name="z_scales%d" % n, align_bytes=64) for n in range(TILES)]
        stats = [const.tile([P, 2, 6], F32, name="stats%d" % c) for c in range(G)]
        turned, grouped, y_ps, mom, mom_ps = {}, {}, {}, {}, {}
        negvar, rstd, scale_pm, shift = {}, {}, {}, {}

        def transposes(n):
            words = z_raw[n][:].rearrange("p s v -> p (s v)").bitcast(F32)
            bank = psum.tile([P, 4, P], F32, name="turned%d" % n, tag=next_bank())
            for g in range(2):
                for u in range(2):
                    nc.tensor.transpose(bank[:, 2 * g + u, :], words[:, 2 * P * g + u:2 * P * (g + 1):2], ident[:])
            turned[n] = bank

        def evacuate(n):
            gt = gpool.tile([P, 2, P, 4], BF16, name="grouped%d" % n, tag="grouped", align_bytes=64)
            nc.scalar.copy(out=gt[:].bitcast(F32), in_=turned[n][:].rearrange("q (g u) r -> q g r u", u=2))
            grouped[n] = gt

        def quantise(n):
            nc.vector.quantize_mx(out=z_codes[n][:].bitcast(FP8X4), scales=z_scales[n][:],
                                  in_=grouped[n][:].rearrange("q g r t -> q (g r t)"))

        def multiply(c, b):
            n = c * B + b
            j = b // 2
            if b % 2 == 0:
                y_ps[c, j] = psum.tile([P, 2 * V], F32, name="y_ps%d_%d" % (c, j), tag="bank%d" % (T_BANKS + (c % 2) * 2 + j))
            c0 = (b % 2) * V
            for g in range(2):
                nc.tensor.matmul_mx(out=y_ps[c, j][:, c0:c0 + V],
                                    lhsT=z_codes[n][:, g * P:(g + 1) * P].bitcast(FP8X4),
                                    lhsT_scale=z_scales[n][:, g * P:(g + 1) * P],
                                    rhs=a_codes[:, g * V:(g + 1) * V].bitcast(FP8X4),
                                    rhs_scale=a_scales[:, g * V:(g + 1) * V],
                                    start=(g == 0), stop=(g == 1))

        def measure(c, j):
            nc.vector.bn_stats(out=stats[c][:, j, :], in_=y_ps[c, j][:])

        def aggregate(c):
            m = small.tile([P, 2], F32, name="mom%d" % c, tag="mom")
            mom[c] = m
            nc.vector.bn_aggr(out=m[:], in_=stats[c][:].rearrange("p j k -> p (j k)"))

        def second_moment(c):
            m = mom[c]
            nc.vector.scalar_tensor_tensor(out=m[:, 1:2], in0=m[:, 0:1], scalar=m[:, 0:1], in1=m[:, 1:2],
                                           op0=ALU.mult, op1=ALU.add)

        def average(c):
            mp = psum.tile([P, 2], F32, name="mom_ps%d" % c, tag=next_bank())
            nc.tensor.matmul(out=mp[:], lhsT=avg[:].rearrange("p o t -> p (o t)"), rhs=mom[c][:], start=True, stop=True)
            mom_ps[c] = mp

        def minus_variance(c):
            nv = small.tile([P, 1], F32, name="negvar%d" % c, tag="negvar")
            nc.vector.tensor_scalar(out=nv[:], in0=mom_ps[c][:, 0:1], scalar1=mom_ps[c][:, 0:1],
                                    scalar2=mom_ps[c][:, 1:2], op0=ALU.mult, op1=ALU.subtract)
            negvar[c] = nv

        def deviation(c):
            rs = small.tile([P, 1], F32, name="rstd%d" % c, tag="rstd")
            nc.scalar.activation(out=rs[:], in_=negvar[c][:], func=ACT.Abs_reciprocal_sqrt, bias=eps_t[:, 0:1], scale=-1.0)
            rstd[c] = rs

        def scales(c):
            sc = small.tile([P, 2], F32, name="scale_pm%d" % c, tag="scale_pm")
            engine = nc.gpsimd if c < G - 1 else nc.vector
            engine.tensor_scalar(out=sc[:], in0=gamma2[:, c, :], scalar1=rstd[c][:, 0:1], scalar2=None, op0=ALU.mult)
            scale_pm[c] = sc

        def shifts(c):
            sh = small.tile([P, 1], F32, name="shift%d" % c, tag="shift")
            nc.scalar.activation(out=sh[:], in_=mom_ps[c][:, 0:1], func=ACT.Identity, bias=gb_pm[:, G + c:G + c + 1],
                                 scale=scale_pm[c][:, 1:2])
            shift[c] = sh

        def normalise(c, j):
            nc.vector.scalar_tensor_tensor(out=res[c][:, j, :], in0=y_ps[c, j][:], scalar=scale_pm[c][:, 0:1],
                                           in1=x_sb[c][:, j, :], op0=ALU.mult, op1=ALU.add)

        def rectify(c, j):
            part = res[c][:, j, :]
            if c == G - 1 and j == BH - 1:
                nc.vector.tensor_scalar(out=part, in0=part, scalar1=shift[c][:, 0:1], scalar2=0.0,
                                        op0=ALU.add, op1=ALU.max)
            else:
                nc.scalar.activation(out=part, in_=part, func=ACT.Relu, bias=shift[c][:, 0:1], scale=1.0)
            for bl in range(BL):
                if c >= G - 2:
                    nc.sync.dma_start(out=ov[c, bl, :, j], in_=res[c][bl::BL, j, :])
                elif j == BH - 1:
                    nc.sync.dma_start(out=ov[c, bl], in_=res[c][bl::BL])

        def keep_warm():
            idle_ps = psum.tile([P, P], F32, name="idle_ps", tag=next_bank())
            for n in range(4):
                nc.tensor.matmul(out=idle_ps[:], lhsT=ident[:], rhs=ident[:], start=True, stop=True)

        turned_to = [0]
        evacuated_to = [0]

        def turn(upto):
            while turned_to[0] < min(upto, TILES):
                transposes(turned_to[0])
                turned_to[0] += 1

        def empty(upto):
            while evacuated_to[0] < min(upto, TILES):
                evacuate(evacuated_to[0])
                evacuated_to[0] += 1

        turn(1)
        empty(1)
        for h in range(G):
            g = h - 1
            if h == 0:
                for n in range(1, B + 1):
                    turn(n + 1)
                    empty(n + 1)
                quantise(0)
                prepare_a()
                for n in range(1, B):
                    quantise(n)
            else:
                if h == G - 1:
                    keep_warm()
                average(g)
                empty(4 * h + 5)
                for b in range(B):
                    quantise(4 * h + b)
                minus_variance(g)
                deviation(g)
                if g > 0:
                    rectify(g - 1, 1)
            for b in range(B):
                multiply(h, b)
            measure(h, 0)
            if h > 0:
                empty(4 * h + 6)
                scales(g)
            measure(h, 1)
            if h == 0:
                spread_matmul()
                spread_out()
            turn(4 * h + LEAD + 1)
            turn(4 * h + LEAD + 2)
            empty(4 * h + 7)
            if h > 0:
                shifts(g)
            turn(4 * h + LEAD + 3)
            empty(4 * h + 8)
            turn(4 * h + LEAD + 4)
            if h < G - 1:
                if h > 0:
                    normalise(g, 0)
                aggregate(h)
                if h > 0:
                    normalise(g, 1)
                    rectify(g, 0)
                second_moment(h)

        g = G - 1
        aggregate(g)
        second_moment(g)
        average(g)
        normalise(g - 1, 0)
        minus_variance(g)
        deviation(g)
        normalise(g - 1, 1)
        rectify(g - 1, 0)
        rectify(g - 1, 1)
        scales(g)
        shifts(g)
        for j in range(2):
            normalise(g, j)
            rectify(g, j)
